import numpy as np
import ml_dtypes


BF16 = ml_dtypes.bfloat16


def bf(x):
    return np.asarray(x, np.float32).astype(BF16)


def f64(x):
    return np.asarray(x).astype(np.float64)


E2M1 = np.array([0.0, 0.5, 1.0, 1.5, 2.0, 3.0, 4.0, 6.0, -0.0, -0.5, -1.0, -1.5, -2.0, -3.0, -4.0, -6.0])


def pack_weight(w, fmt):
    k, n = w.shape
    w = f64(bf(w)).reshape(k // 32, 32, n)
    amax = np.abs(w).max(1)
    if fmt == "e4m3":
        byte = np.frexp(amax)[1] - 1 + 127 - 7
    else:
        mant, ex = np.frexp(amax / 6.0)
        byte = np.where(mant > 0.5, ex, ex - 1) + 127
    byte = np.clip(np.where(amax > 0, byte, 1), 1, 254)
    scaled = (w * np.exp2(127.0 - byte)[:, None, :]).reshape(k, n).astype(np.float32)
    by_word = np.ascontiguousarray(scaled.reshape(k // 512, 128, 4, n).transpose(0, 1, 3, 2))
    if fmt == "e4m3":
        words = by_word.astype(ml_dtypes.float8_e4m3fn).view(np.uint8)
    else:
        c = by_word.astype(ml_dtypes.float4_e2m1fn).view(np.uint8) & 0xF
        words = c[..., 0::2] | (c[..., 1::2] << 4)
    return np.ascontiguousarray(words), np.ascontiguousarray(byte.astype(np.uint8).reshape(k // 512, 16, n))


def unpack_weight(words, scales, fmt):
    g, p, n, _ = words.shape
    if fmt == "e4m3":
        vals = np.ascontiguousarray(words).view(ml_dtypes.float8_e4m3fn).astype(np.float64)
    else:
        nib = np.empty((g, p, n, 4), np.uint8)
        nib[..., 0::2] = words & 0xF
        nib[..., 1::2] = words >> 4
        vals = E2M1[nib]
    vals = vals * np.repeat(np.exp2(scales.astype(np.float64) - 127.0), 8, axis=1)[..., None]
    return vals.transpose(0, 1, 3, 2).reshape(g * 512, n)

def pack4(w):
    words, scales = pack_weight(w, "e2m1")
    return words.reshape(words.shape[0], 128, -1), scales


def unpack4(words, scales):
    return unpack_weight(words.reshape(words.shape[0], 128, -1, 2), scales, "e2m1")


def kspread(k):
    return np.exp2(np.repeat(np.random.randint(-6, 7, k // 32), 32).astype(np.float64))


B, T, D, H = 1, 512, 2048, 16
HD = D // H
SCALE = HD ** (-0.5)


def rotate_half(u):
    u1, u2 = np.split(u, 2, axis=-1)
    return np.concatenate([-u2, u1], axis=-1)


def apply_rope(u, sin, cos):
    return u * cos[None, :, None, :] + rotate_half(u) * sin[None, :, None, :]


def setup_inputs():
    s = kspread(D)
    x = np.random.standard_normal((B, T, D)) * s
    x_words, x_scales = pack4(np.ascontiguousarray(x.reshape(B * T, D).T))
    sin = bf(np.random.standard_normal((T, HD)))
    cos = bf(np.random.standard_normal((T, HD)))
    words, scales = pack4(np.random.standard_normal((D, D + 2 * HD)) * 2.0 / np.sqrt(D) / s[:, None])
    return {"x_words": x_words,
            "x_scales": x_scales,
            "sin": sin,
            "cos": cos,
            "W_qkv_words": words,
            "W_qkv_scales": scales}


def reference(x_words, x_scales, sin, cos, W_qkv_words, W_qkv_scales):
    sin, cos = f64(sin), f64(cos)
    x = unpack4(x_words, x_scales).T.reshape(B, T, D)
    qkv = x @ unpack4(W_qkv_words, W_qkv_scales)
    q, k, v = np.split(qkv, [D, D + HD], axis=-1)
    q = q.reshape(B, T, H, HD) * SCALE
    q_rot = np.ascontiguousarray(apply_rope(q, sin, cos).transpose(0, 2, 1, 3))
    k_rot = apply_rope(k[:, :, None, :], sin, cos)[:, :, 0, :]
    return q_rot, k_rot, v

@@ -1,0 +1,192 @@
+from contextlib import ExitStack
+
+import concourse.mybir as mybir
+
+F32 = mybir.dt.float32
+BF16 = mybir.dt.bfloat16
+I32 = mybir.dt.int32
+U8 = mybir.dt.uint8
+FP4X4 = mybir.dt.float4_e2m1fn_x4
+MULT = mybir.AluOpType.mult
+ADD = mybir.AluOpType.add
+COPY = mybir.ActivationFunctionType.Copy
+
+P = 128
+T = 512
+D = 2048
+HD = 128
+HALF = 64
+G = 4
+MT = 4
+QC = 4
+SCALE = HD ** -0.5
+FLOPS = 2 * T * D * (D + 2 * HD)
+
+WARM = 8
+MERGED_B = True
+
+UNITS = [
+    [("g", [(0, 0, 2)]), ("g", [(0, 2, 2)]), ("g", [(1, 0, 4)]), ("g", [(2, 0, 4), (3, 0, 4)])],
+    [("g", [(0, 0, 4), (1, 0, 4)]), ("g", [(2, 0, 4), (3, 0, 4)])],
+    [("g", [(0, 0, 4), (1, 0, 4)]), ("g", [(2, 0, 4), (3, 0, 4)])],
+    [("g", [(0, 0, 4), (1, 0, 4)]), ("g", [(2, 0, 4)]), ("v", [(3, 0, 4)])],
+]
+
+
+def tile_multiqueryattention_pa_kernel(
+    tc, x_words, x_scales, sin, cos, W_qkv_words, W_qkv_scales, out_0, out_1, out_2
+):
+    nc = tc.nc
+    with ExitStack() as ctx:
+        sb = ctx.enter_context(tc.tile_pool(name="sb", bufs=1))
+        ps = ctx.enter_context(tc.psum_pool(name="ps", bufs=8))
+        ctx.enter_context(tc.manual_schedule())
+
+        xc = sb.tile([P, G, 2 * T], U8, name="xc", align_bytes=64)
+        xs = sb.tile([P, G, T], U8, name="xs", align_bytes=64)
+        wc = [sb.tile([P, G, 1024], U8, name="wc%d" % c, align_bytes=64) for c in range(QC)]
+        wckv = sb.tile([P, G, 512], U8, name="wckv", align_bytes=64)
+        ws0 = sb.tile([P, G, 512], U8, name="ws0", align_bytes=64)
+        wsr = sb.tile([P, G, 1792], U8, name="wsr", align_bytes=64)
+        cos_raw = sb.tile([P, MT, HD], BF16, name="cos_raw")
+        sin_raw = sb.tile([P, MT, HD], BF16, name="sin_raw")
+        cosq = sb.tile([P, MT, HD], F32, name="cosq")
+        sinq = sb.tile([P, MT, HD], F32, name="sinq")
+        sink = sb.tile([P, MT, HD], F32, name="sink")
+        zero = sb.tile([P, 512], BF16, name="zero")
+        scr = sb.tile([P, 8], F32, name="scr")
+
+        nc.vector.memset(zero[:], 0.0)
+        nc.vector.memset(xs[:].bitcast(I32), 0)
+        nc.vector.memset(ws0[:].bitcast(I32), 0)
+        nc.vector.memset(wsr[:].bitcast(I32), 0)
+
+        nc.gpsimd.dma_start(out=cos_raw[:], in_=cos.rearrange("(m p) d -> p m d", p=P))
+        nc.gpsimd.dma_start(out=sin_raw[:], in_=sin.rearrange("(m p) d -> p m d", p=P))
+
+        def load_codes(tile_ap, words, lo, hi):
+            nc.sync.dma_start(
+                out=tile_ap.bitcast(I32),
+                in_=words[:, :, lo:hi].rearrange("g p n -> p g n").bitcast(I32),
+            )
+
+        def load_scales(plane, scales, lo, hi):
+            for q in range(4):
+                nc.sync.dma_start(
+                    out=plane[32 * q : 32 * q + 4, :, :].bitcast(I32),
+                    in_=scales[:, 4 * q : 4 * q + 4, lo:hi].rearrange("g r n -> r g n").bitcast(I32),
+                )
+
+        load_codes(xc[:], x_words, 0, 1024)
+        load_codes(wc[0][:], W_qkv_words, 0, 1024)
+        load_scales(xs, x_scales, 0, 512)
+        load_scales(ws0, W_qkv_scales, 0, 512)
+        load_scales(wsr, W_qkv_scales, 512, 2304)
+        for c in range(1, QC):
+            load_codes(wc[c][:], W_qkv_words, 1024 * c, 1024 * (c + 1))
+        load_codes(wckv[:], W_qkv_words, 4096, 4608)
+
+        if WARM:
+            warm = ps.tile([P, 512], F32, tag="acc", name="warm")
+            for i in range(WARM):
+                nc.tensor.matmul(out=warm[:], lhsT=zero[:, 0:P], rhs=zero[:], start=True, stop=True)
+
+        nc.scalar.activation(out=scr[:, 0:1], in_=zero[:, 0:1], func=COPY, scale=1.0)
+        nc.scalar.activation(out=cosq[:], in_=cos_raw[:], func=COPY, scale=SCALE)
+        nc.scalar.activation(out=sinq[:, :, 0:HALF], in_=sin_raw[:, :, 0:HALF], func=COPY, scale=-SCALE)
+        nc.scalar.activation(out=sinq[:, :, HALF:HD], in_=sin_raw[:, :, HALF:HD], func=COPY, scale=SCALE)
+        nc.scalar.activation(out=sink[:, :, 0:HALF], in_=sin_raw[:, :, 0:HALF], func=COPY, scale=-1.0)
+        nc.scalar.activation(out=sink[:, :, HALF:HD], in_=sin_raw[:, :, HALF:HD], func=COPY, scale=1.0)
+
+        def project(acc, m, codes, plane, col, n):
+            for g in range(G):
+                nc.tensor.matmul_mx(
+                    out=acc,
+                    lhsT=xc[:, g, 256 * m : 256 * (m + 1)].bitcast(FP4X4),
+                    lhsT_scale=xs[:, g, P * m : P * (m + 1)],
+                    rhs=codes[:, g, 2 * col[0] : 2 * (col[0] + n)].bitcast(FP4X4),
+                    rhs_scale=plane[:, g, col[1] : col[1] + n],
+                    start=(g == 0),
+                    stop=(g == G - 1),
+                )
+
+        def rope_products(acc, a, b, cos_t, sin_t):
+            nb = acc.shape[1]
+            nc.vector.tensor_tensor(out=a, in0=acc, in1=cos_t, op=MULT)
+            if MERGED_B:
+                nc.vector.tensor_tensor(
+                    out=b.rearrange("p h (s d) -> p h s d", s=2),
+                    in0=acc.rearrange("p h (s d) -> p h s d", s=2)[:, :, ::-1, :],
+                    in1=sin_t.rearrange("p h (s d) -> p h s d", s=2),
+                    op=MULT,
+                )
+            else:
+                nc.vector.tensor_tensor(
+                    out=b[:, :, 0:HALF], in0=acc[:, :, HALF:HD], in1=sin_t[:, :, 0:HALF], op=MULT
+                )
+                nc.vector.tensor_tensor(
+                    out=b[:, :, HALF:HD], in0=acc[:, :, 0:HALF], in1=sin_t[:, :, HALF:HD], op=MULT
+                )
+
+        def blocks(ap):
+            return ap.rearrange("p (h d) -> p h d", d=HD)
+
+        def queries(c):
+            codes = wc[c]
+            plane = ws0 if c == 0 else wsr
+            base = 0 if c == 0 else 512 * (c - 1)
+            for ui, unit in enumerate(UNITS[c]):
+                eng, parts = unit
+                width = HD * sum(nh for (m, h0, nh) in parts)
+                a = sb.tile([P, width], F32, name="a%d_%d" % (c, ui))
+                b = sb.tile([P, width], F32, name="b%d_%d" % (c, ui))
+                o = sb.tile([P, width], F32, name="o%d_%d" % (c, ui))
+                off = 0
+                for (m, h0, nh) in parts:
+                    n = HD * nh
+                    acc = ps.tile([P, n], F32, tag="acc", name="acc%d_%d_%d" % (c, m, h0))
+                    project(acc[:], m, codes, plane, (HD * h0, base + HD * h0), n)
+                    rope_products(
+                        blocks(acc[:]), blocks(a[:, off : off + n]), blocks(b[:, off : off + n]),
+                        cosq[:, m, :].unsqueeze(1).to_broadcast([P, nh, HD]),
+                        sinq[:, m, :].unsqueeze(1).to_broadcast([P, nh, HD]),
+                    )
+                    off += n
+                if eng == "v":
+                    nc.vector.tensor_tensor(out=o[:], in0=a[:], in1=b[:], op=ADD)
+                else:
+                    nc.gpsimd.tensor_tensor(out=o[:], in0=a[:], in1=b[:], op=ADD)
+                off = 0
+                for (m, h0, nh) in parts:
+                    n = HD * nh
+                    nc.sync.dma_start(
+                        out=out_0[0, 4 * c + h0 : 4 * c + h0 + nh, P * m : P * (m + 1), :].rearrange("h p d -> p h d"),
+                        in_=blocks(o[:, off : off + n]),
+                    )
+                    off += n
+
+        def keys():
+            acc = ps.tile([P, 512], F32, tag="acc", name="acc_k")
+            for m in range(MT):
+                project(acc[:, HD * m : HD * (m + 1)], m, wckv, wsr, (0, 1536), HD)
+            a = sb.tile([P, 512], F32, name="ak")
+            b = sb.tile([P, 512], F32, name="bk")
+            o = sb.tile([P, 512], F32, name="ok")
+            rope_products(blocks(acc[:]), blocks(a[:]), blocks(b[:]), cos_raw[:], sink[:])
+            nc.gpsimd.tensor_tensor(out=o[:], in0=a[:], in1=b[:], op=ADD)
+            nc.scalar.dma_start(out=out_1[0].rearrange("(m p) d -> p m d", p=P), in_=blocks(o[:]))
+
+        def values():
+            acc = ps.tile([P, 512], F32, tag="acc", name="acc_v")
+            for m in range(MT):
+                project(acc[:, HD * m : HD * (m + 1)], m, wckv, wsr, (HD, 1664), HD)
+            o = sb.tile([P, 512], F32, name="ov")
+            nc.scalar.copy(out=o[:], in_=acc[:])
+            nc.scalar.dma_start(out=out_2[0].rearrange("(m p) d -> p m d", p=P), in_=blocks(o[:]))
+
+        queries(0)
+        queries(1)
+        queries(2)
+        keys()
+        queries(3)
+        values()

@@ -22,7 +22,7 @@ QC = 4
 SCALE = HD ** -0.5
 FLOPS = 2 * T * D * (D + 2 * HD)
 
-WARM = 8
+WARM = 12
 MERGED_B = True
 
 UNITS = [
@@ -42,7 +42,8 @@ def tile_multiqueryattention_pa_kernel(
         ps = ctx.enter_context(tc.psum_pool(name="ps", bufs=8))
         ctx.enter_context(tc.manual_schedule())
 
-        xc = sb.tile([P, G, 2 * T], U8, name="xc", align_bytes=64)
+        xc0 = sb.tile([P, G, 256], U8, name="xc0", align_bytes=64)
+        xcr = sb.tile([P, G, 768], U8, name="xcr", align_bytes=64)
         xs = sb.tile([P, G, T], U8, name="xs", align_bytes=64)
         wc = [sb.tile([P, G, 1024], U8, name="wc%d" % c, align_bytes=64) for c in range(QC)]
         wckv = sb.tile([P, G, 512], U8, name="wckv", align_bytes=64)
@@ -55,14 +56,16 @@ def tile_multiqueryattention_pa_kernel(
         sink = sb.tile([P, MT, HD], F32, name="sink")
         zero = sb.tile([P, 512], BF16, name="zero")
         scr = sb.tile([P, 8], F32, name="scr")
+        scrg = sb.tile([P, 8], F32, name="scrg")
 
         nc.vector.memset(zero[:], 0.0)
         nc.vector.memset(xs[:].bitcast(I32), 0)
         nc.vector.memset(ws0[:].bitcast(I32), 0)
-        nc.vector.memset(wsr[:].bitcast(I32), 0)
 
-        nc.gpsimd.dma_start(out=cos_raw[:], in_=cos.rearrange("(m p) d -> p m d", p=P))
-        nc.gpsimd.dma_start(out=sin_raw[:], in_=sin.rearrange("(m p) d -> p m d", p=P))
+
+        nc.gpsimd.memset(wsr[:].bitcast(F32), 0.0)
+
+        nc.gpsimd.tensor_tensor(out=scrg[:], in0=zero[:, 0:8], in1=zero[:, 8:16], op=ADD)
 
         def load_codes(tile_ap, words, lo, hi):
             nc.sync.dma_start(
@@ -70,17 +73,20 @@ def tile_multiqueryattention_pa_kernel(
                 in_=words[:, :, lo:hi].rearrange("g p n -> p g n").bitcast(I32),
             )
 
-        def load_scales(plane, scales, lo, hi):
-            for q in range(4):
+        def load_scales(plane, scales, lo, hi, quads=(0, 1, 2, 3)):
+            for q in quads:
                 nc.sync.dma_start(
                     out=plane[32 * q : 32 * q + 4, :, :].bitcast(I32),
                     in_=scales[:, 4 * q : 4 * q + 4, lo:hi].rearrange("g r n -> r g n").bitcast(I32),
                 )
 
-        load_codes(xc[:], x_words, 0, 1024)
-        load_codes(wc[0][:], W_qkv_words, 0, 1024)
+        load_codes(xc0[:], x_words, 0, 256)
+        nc.scalar.dma_start(out=cos_raw[:], in_=cos.rearrange("(m p) d -> p m d", p=P))
+        nc.scalar.dma_start(out=sin_raw[:], in_=sin.rearrange("(m p) d -> p m d", p=P))
         load_scales(xs, x_scales, 0, 512)
+        load_codes(wc[0][:], W_qkv_words, 0, 1024)
         load_scales(ws0, W_qkv_scales, 0, 512)
+        load_codes(xcr[:], x_words, 256, 1024)
         load_scales(wsr, W_qkv_scales, 512, 2304)
         for c in range(1, QC):
             load_codes(wc[c][:], W_qkv_words, 1024 * c, 1024 * (c + 1))
@@ -102,7 +108,7 @@ def tile_multiqueryattention_pa_kernel(
             for g in range(G):
                 nc.tensor.matmul_mx(
                     out=acc,
-                    lhsT=xc[:, g, 256 * m : 256 * (m + 1)].bitcast(FP4X4),
+                    lhsT=(xc0[:, g, :] if m == 0 else xcr[:, g, 256 * (m - 1) : 256 * m]).bitcast(FP4X4),
                     lhsT_scale=xs[:, g, P * m : P * (m + 1)],
                     rhs=codes[:, g, 2 * col[0] : 2 * (col[0] + n)].bitcast(FP4X4),
                     rhs_scale=plane[:, g, col[1] : col[1] + n],

@@ -56,16 +56,11 @@ def tile_multiqueryattention_pa_kernel(
         sink = sb.tile([P, MT, HD], F32, name="sink")
         zero = sb.tile([P, 512], BF16, name="zero")
         scr = sb.tile([P, 8], F32, name="scr")
-        scrg = sb.tile([P, 8], F32, name="scrg")
 
-        nc.vector.memset(zero[:], 0.0)
         nc.vector.memset(xs[:].bitcast(I32), 0)
+        nc.vector.memset(zero[:], 0.0)
         nc.vector.memset(ws0[:].bitcast(I32), 0)
-
-
-        nc.gpsimd.memset(wsr[:].bitcast(F32), 0.0)
-
-        nc.gpsimd.tensor_tensor(out=scrg[:], in0=zero[:, 0:8], in1=zero[:, 8:16], op=ADD)
+        nc.vector.memset(wsr[:].bitcast(I32), 0)
 
         def load_codes(tile_ap, words, lo, hi):
             nc.sync.dma_start(

@@ -23,7 +23,6 @@ SCALE = HD ** -0.5
 FLOPS = 2 * T * D * (D + 2 * HD)
 
 WARM = 12
-MERGED_B = True
 
 UNITS = [
     [("g", [(0, 0, 2)]), ("g", [(0, 2, 2)]), ("g", [(1, 0, 4)]), ("g", [(2, 0, 4), (3, 0, 4)])],
@@ -51,9 +50,8 @@ def tile_multiqueryattention_pa_kernel(
         wsr = sb.tile([P, G, 1792], U8, name="wsr", align_bytes=64)
         cos_raw = sb.tile([P, MT, HD], BF16, name="cos_raw")
         sin_raw = sb.tile([P, MT, HD], BF16, name="sin_raw")
-        cosq = sb.tile([P, MT, HD], F32, name="cosq")
-        sinq = sb.tile([P, MT, HD], F32, name="sinq")
-        sink = sb.tile([P, MT, HD], F32, name="sink")
+        tabq = sb.tile([P, MT, 2, HD], F32, name="tabq")
+        tabk = sb.tile([P, MT, 2, HD], F32, name="tabk")
         zero = sb.tile([P, 512], BF16, name="zero")
         scr = sb.tile([P, 8], F32, name="scr")
 
@@ -93,11 +91,10 @@ def tile_multiqueryattention_pa_kernel(
                 nc.tensor.matmul(out=warm[:], lhsT=zero[:, 0:P], rhs=zero[:], start=True, stop=True)
 
         nc.scalar.activation(out=scr[:, 0:1], in_=zero[:, 0:1], func=COPY, scale=1.0)
-        nc.scalar.activation(out=cosq[:], in_=cos_raw[:], func=COPY, scale=SCALE)
-        nc.scalar.activation(out=sinq[:, :, 0:HALF], in_=sin_raw[:, :, 0:HALF], func=COPY, scale=-SCALE)
-        nc.scalar.activation(out=sinq[:, :, HALF:HD], in_=sin_raw[:, :, HALF:HD], func=COPY, scale=SCALE)
-        nc.scalar.activation(out=sink[:, :, 0:HALF], in_=sin_raw[:, :, 0:HALF], func=COPY, scale=-1.0)
-        nc.scalar.activation(out=sink[:, :, HALF:HD], in_=sin_raw[:, :, HALF:HD], func=COPY, scale=1.0)
+        for (tab, f) in ((tabq, SCALE), (tabk, 1.0)):
+            nc.scalar.activation(out=tab[:, :, 0, :], in_=cos_raw[:], func=COPY, scale=f)
+            nc.scalar.activation(out=tab[:, :, 1, 0:HALF], in_=sin_raw[:, :, HALF:HD], func=COPY, scale=f)
+            nc.scalar.activation(out=tab[:, :, 1, HALF:HD], in_=sin_raw[:, :, 0:HALF], func=COPY, scale=-f)
 
         def project(acc, m, codes, plane, col, n):
             for g in range(G):
@@ -111,26 +108,20 @@ def tile_multiqueryattention_pa_kernel(
                     stop=(g == G - 1),
                 )
 
-        def rope_products(acc, a, b, cos_t, sin_t):
-            nb = acc.shape[1]
-            nc.vector.tensor_tensor(out=a, in0=acc, in1=cos_t, op=MULT)
-            if MERGED_B:
-                nc.vector.tensor_tensor(
-                    out=b.rearrange("p h (s d) -> p h s d", s=2),
-                    in0=acc.rearrange("p h (s d) -> p h s d", s=2)[:, :, ::-1, :],
-                    in1=sin_t.rearrange("p h (s d) -> p h s d", s=2),
-                    op=MULT,
-                )
-            else:
-                nc.vector.tensor_tensor(
-                    out=b[:, :, 0:HALF], in0=acc[:, :, HALF:HD], in1=sin_t[:, :, 0:HALF], op=MULT
-                )
-                nc.vector.tensor_tensor(
-                    out=b[:, :, HALF:HD], in0=acc[:, :, 0:HALF], in1=sin_t[:, :, HALF:HD], op=MULT
-                )
-
         def blocks(ap):
             return ap.rearrange("p (h d) -> p h d", d=HD)
+
+        def products(acc, ab, tab):
+            nb = acc.shape[1]
+            nc.vector.tensor_tensor(out=ab, in0=acc.unsqueeze(2).to_broadcast([P, nb, 2, HD]), in1=tab, op=MULT)
+
+        def halves(ap):
+            return ap.rearrange("p h (s d) -> p h s d", s=2)
+
+        def rope_sum(eng, o, ab):
+            eng.tensor_tensor(
+                out=halves(o), in0=halves(ab[:, :, 0, :]), in1=halves(ab[:, :, 1, :])[:, :, ::-1, :], op=ADD
+            )
 
         def queries(c):
             codes = wc[c]
@@ -138,44 +129,37 @@ def tile_multiqueryattention_pa_kernel(
             base = 0 if c == 0 else 512 * (c - 1)
             for ui, unit in enumerate(UNITS[c]):
                 eng, parts = unit
-                width = HD * sum(nh for (m, h0, nh) in parts)
-                a = sb.tile([P, width], F32, name="a%d_%d" % (c, ui))
-                b = sb.tile([P, width], F32, name="b%d_%d" % (c, ui))
-                o = sb.tile([P, width], F32, name="o%d_%d" % (c, ui))
+                heads = sum(nh for (m, h0, nh) in parts)
+                ab = sb.tile([P, heads, 2, HD], F32, name="ab%d_%d" % (c, ui))
+                o = sb.tile([P, heads, HD], F32, name="o%d_%d" % (c, ui))
                 off = 0
                 for (m, h0, nh) in parts:
                     n = HD * nh
                     acc = ps.tile([P, n], F32, tag="acc", name="acc%d_%d_%d" % (c, m, h0))
                     project(acc[:], m, codes, plane, (HD * h0, base + HD * h0), n)
-                    rope_products(
-                        blocks(acc[:]), blocks(a[:, off : off + n]), blocks(b[:, off : off + n]),
-                        cosq[:, m, :].unsqueeze(1).to_broadcast([P, nh, HD]),
-                        sinq[:, m, :].unsqueeze(1).to_broadcast([P, nh, HD]),
+                    products(
+                        blocks(acc[:]), ab[:, off : off + nh, :, :],
+                        tabq[:, m, :, :].unsqueeze(1).to_broadcast([P, nh, 2, HD]),
                     )
-                    off += n
-                if eng == "v":
-                    nc.vector.tensor_tensor(out=o[:], in0=a[:], in1=b[:], op=ADD)
-                else:
-                    nc.gpsimd.tensor_tensor(out=o[:], in0=a[:], in1=b[:], op=ADD)
+                    off += nh
+                rope_sum(nc.vector if eng == "v" else nc.gpsimd, o[:], ab)
                 off = 0
                 for (m, h0, nh) in parts:
-                    n = HD * nh
                     nc.sync.dma_start(
                         out=out_0[0, 4 * c + h0 : 4 * c + h0 + nh, P * m : P * (m + 1), :].rearrange("h p d -> p h d"),
-                        in_=blocks(o[:, off : off + n]),
+                        in_=o[:, off : off + nh, :],
                     )
-                    off += n
+                    off += nh
 
         def keys():
             acc = ps.tile([P, 512], F32, tag="acc", name="acc_k")
             for m in range(MT):
                 project(acc[:, HD * m : HD * (m + 1)], m, wckv, wsr, (0, 1536), HD)
-            a = sb.tile([P, 512], F32, name="ak")
-            b = sb.tile([P, 512], F32, name="bk")
-            o = sb.tile([P, 512], F32, name="ok")
-            rope_products(blocks(acc[:]), blocks(a[:]), blocks(b[:]), cos_raw[:], sink[:])
-            nc.gpsimd.tensor_tensor(out=o[:], in0=a[:], in1=b[:], op=ADD)
-            nc.scalar.dma_start(out=out_1[0].rearrange("(m p) d -> p m d", p=P), in_=blocks(o[:]))
+            ab = sb.tile([P, MT, 2, HD], F32, name="abk")
+            o = sb.tile([P, MT, HD], F32, name="ok")
+            products(blocks(acc[:]), ab[:], tabk[:])
+            rope_sum(nc.gpsimd, o[:], ab)
+            nc.scalar.dma_start(out=out_1[0].rearrange("(m p) d -> p m d", p=P), in_=o[:])
 
         def values():
             acc = ps.tile([P, 512], F32, tag="acc", name="acc_v")

@@ -24,11 +24,41 @@ FLOPS = 2 * T * D * (D + 2 * HD)
 
 WARM = 12
 
-UNITS = [
-    [("g", [(0, 0, 2)]), ("g", [(0, 2, 2)]), ("g", [(1, 0, 4)]), ("g", [(2, 0, 4), (3, 0, 4)])],
-    [("g", [(0, 0, 4), (1, 0, 4)]), ("g", [(2, 0, 4), (3, 0, 4)])],
-    [("g", [(0, 0, 4), (1, 0, 4)]), ("g", [(2, 0, 4), (3, 0, 4)])],
-    [("g", [(0, 0, 4), (1, 0, 4)]), ("g", [(2, 0, 4)]), ("v", [(3, 0, 4)])],
+STEPS = [
+    ("q", "a", 0, 0, 0, 2),
+    ("sum", "g", "a", "s"),
+    ("q", "b", 0, 0, 2, 2),
+    ("sum", "g", "b", "s"),
+    ("q", "c", 0, 1, 0, 4),
+    ("sum", "g", "c", "s"),
+    ("q", "d", 0, 2, 0, 4),
+    ("q", "d", 0, 3, 0, 4),
+    ("sum", "g", "d", "s"),
+    ("q", "e", 1, 0, 0, 4),
+    ("q", "e", 1, 1, 0, 4),
+    ("sum", "g", "e", "s"),
+    ("q", "f", 1, 2, 0, 4),
+    ("q", "f", 1, 3, 0, 4),
+    ("sum", "g", "f", "s"),
+    ("q", "g", 2, 0, 0, 4),
+    ("q", "g", 2, 1, 0, 4),
+    ("sum", "g", "g", "s"),
+    ("q", "h", 2, 2, 0, 4),
+    ("q", "h", 2, 3, 0, 4),
+    ("sum", "g", "h", "s"),
+    ("k", "k"),
+    ("sum", "g", "k", "a"),
+    ("q", "i", 3, 0, 0, 4),
+    ("sum", "g", "i", "s"),
+    ("q", "m", 3, 1, 0, 4),
+    ("q", "j", 3, 2, 0, 4),
+    ("q", "l", 3, 3, 0, 2),
+    ("q", "n", 3, 3, 2, 2),
+    ("v",),
+    ("sum", "v", "m", "s"),
+    ("sum", "v", "j", "a"),
+    ("sum", "v", "l", "s"),
+    ("sum", "v", "n", "a"),
 ]
 
 
@@ -123,55 +153,60 @@ def tile_multiqueryattention_pa_kernel(
                 out=halves(o), in0=halves(ab[:, :, 0, :]), in1=halves(ab[:, :, 1, :])[:, :, ::-1, :], op=ADD
             )
 
-        def queries(c):
-            codes = wc[c]
-            plane = ws0 if c == 0 else wsr
-            base = 0 if c == 0 else 512 * (c - 1)
-            for ui, unit in enumerate(UNITS[c]):
-                eng, parts = unit
-                heads = sum(nh for (m, h0, nh) in parts)
-                ab = sb.tile([P, heads, 2, HD], F32, name="ab%d_%d" % (c, ui))
-                o = sb.tile([P, heads, HD], F32, name="o%d_%d" % (c, ui))
-                off = 0
-                for (m, h0, nh) in parts:
-                    n = HD * nh
-                    acc = ps.tile([P, n], F32, tag="acc", name="acc%d_%d_%d" % (c, m, h0))
-                    project(acc[:], m, codes, plane, (HD * h0, base + HD * h0), n)
-                    products(
-                        blocks(acc[:]), ab[:, off : off + nh, :, :],
-                        tabq[:, m, :, :].unsqueeze(1).to_broadcast([P, nh, 2, HD]),
-                    )
-                    off += nh
-                rope_sum(nc.vector if eng == "v" else nc.gpsimd, o[:], ab)
-                off = 0
-                for (m, h0, nh) in parts:
-                    nc.sync.dma_start(
-                        out=out_0[0, 4 * c + h0 : 4 * c + h0 + nh, P * m : P * (m + 1), :].rearrange("h p d -> p h d"),
-                        in_=o[:, off : off + nh, :],
-                    )
-                    off += nh
-
-        def keys():
-            acc = ps.tile([P, 512], F32, tag="acc", name="acc_k")
-            for m in range(MT):
-                project(acc[:, HD * m : HD * (m + 1)], m, wckv, wsr, (0, 1536), HD)
-            ab = sb.tile([P, MT, 2, HD], F32, name="abk")
-            o = sb.tile([P, MT, HD], F32, name="ok")
-            products(blocks(acc[:]), ab[:], tabk[:])
-            rope_sum(nc.gpsimd, o[:], ab)
-            nc.scalar.dma_start(out=out_1[0].rearrange("(m p) d -> p m d", p=P), in_=o[:])
-
-        def values():
-            acc = ps.tile([P, 512], F32, tag="acc", name="acc_v")
-            for m in range(MT):
-                project(acc[:, HD * m : HD * (m + 1)], m, wckv, wsr, (HD, 1664), HD)
-            o = sb.tile([P, 512], F32, name="ov")
-            nc.scalar.copy(out=o[:], in_=acc[:])
-            nc.scalar.dma_start(out=out_2[0].rearrange("(m p) d -> p m d", p=P), in_=blocks(o[:]))
-
-        queries(0)
-        queries(1)
-        queries(2)
-        keys()
-        queries(3)
-        values()
+        size = {}
+        for st in STEPS:
+            if st[0] == "q":
+                size[st[1]] = size.get(st[1], 0) + st[5]
+            elif st[0] == "k":
+                size[st[1]] = MT
+        tiles = {}
+        parts = {}
+        for st in STEPS:
+            if st[0] == "q":
+                (kind, u, c, m, h0, nh) = st
+                if u not in tiles:
+                    tiles[u] = sb.tile([P, size[u], 2, HD], F32, name="ab_%s" % u)
+                    parts[u] = []
+                off = sum(p[3] for p in parts[u])
+                parts[u].append((c, m, h0, nh))
+                acc = ps.tile([P, HD * nh], F32, tag="acc", name="acc%d_%d_%d" % (c, m, h0))
+                project(
+                    acc[:], m, wc[c], ws0 if c == 0 else wsr,
+                    (HD * h0, HD * h0 if c == 0 else 512 * (c - 1) + HD * h0), HD * nh,
+                )
+                products(
+                    blocks(acc[:]), tiles[u][:, off : off + nh, :, :],
+                    tabq[:, m, :, :].unsqueeze(1).to_broadcast([P, nh, 2, HD]),
+                )
+            elif st[0] == "k":
+                u = st[1]
+                tiles[u] = sb.tile([P, MT, 2, HD], F32, name="ab_%s" % u)
+                parts[u] = None
+                acc = ps.tile([P, 512], F32, tag="acc", name="acc_k")
+                for m in range(MT):
+                    project(acc[:, HD * m : HD * (m + 1)], m, wckv, wsr, (0, 1536), HD)
+                products(blocks(acc[:]), tiles[u][:], tabk[:])
+            elif st[0] == "v":
+                acc = ps.tile([P, 512], F32, tag="acc", name="acc_v")
+                for m in range(MT):
+                    project(acc[:, HD * m : HD * (m + 1)], m, wckv, wsr, (HD, 1664), HD)
+                ov = sb.tile([P, 512], F32, name="ov")
+                nc.scalar.copy(out=ov[:], in_=acc[:])
+                nc.scalar.dma_start(out=out_2[0].rearrange("(m p) d -> p m d", p=P), in_=blocks(ov[:]))
+            else:
+                (kind, eng, u, qu) = st
+                dma = nc.sync if qu == "s" else nc.scalar
+                o = sb.tile([P, size[u], HD], F32, name="o_%s" % u)
+                rope_sum(nc.vector if eng == "v" else nc.gpsimd, o[:], tiles[u])
+                if parts[u] is None:
+                    dma.dma_start(out=out_1[0].rearrange("(m p) d -> p m d", p=P), in_=o[:])
+                else:
+                    off = 0
+                    for (c, m, h0, nh) in parts[u]:
+                        dma.dma_start(
+                            out=out_0[0, 4 * c + h0 : 4 * c + h0 + nh, P * m : P * (m + 1), :].rearrange(
+                                "h p d -> p h d"
+                            ),
+                            in_=o[:, off : off + nh, :],
+                        )
+                        off += nh

@@ -32,8 +32,9 @@ STEPS = [
     ("q", "c", 0, 1, 0, 4),
     ("sum", "g", "c", "s"),
     ("q", "d", 0, 2, 0, 4),
-    ("q", "d", 0, 3, 0, 4),
     ("sum", "g", "d", "s"),
+    ("q", "p", 0, 3, 0, 4),
+    ("sum", "g", "p", "s"),
     ("q", "e", 1, 0, 0, 4),
     ("q", "e", 1, 1, 0, 4),
     ("sum", "g", "e", "s"),
@@ -51,13 +52,13 @@ STEPS = [
     ("q", "i", 3, 0, 0, 4),
     ("sum", "g", "i", "s"),
     ("q", "m", 3, 1, 0, 4),
+    ("sum", "g", "m", "s"),
     ("q", "j", 3, 2, 0, 4),
     ("q", "l", 3, 3, 0, 2),
     ("q", "n", 3, 3, 2, 2),
     ("v",),
-    ("sum", "v", "m", "s"),
     ("sum", "v", "j", "a"),
-    ("sum", "v", "l", "s"),
+    ("sum", "v", "l", "a"),
     ("sum", "v", "n", "a"),
 ]
 
@@ -77,7 +78,8 @@ def tile_multiqueryattention_pa_kernel(
         wc = [sb.tile([P, G, 1024], U8, name="wc%d" % c, align_bytes=64) for c in range(QC)]
         wckv = sb.tile([P, G, 512], U8, name="wckv", align_bytes=64)
         ws0 = sb.tile([P, G, 512], U8, name="ws0", align_bytes=64)
-        wsr = sb.tile([P, G, 1792], U8, name="wsr", align_bytes=64)
+        ws1 = sb.tile([P, G, 512], U8, name="ws1", align_bytes=64)
+        wsr = sb.tile([P, G, 1280], U8, name="wsr", align_bytes=64)
         cos_raw = sb.tile([P, MT, HD], BF16, name="cos_raw")
         sin_raw = sb.tile([P, MT, HD], BF16, name="sin_raw")
         tabq = sb.tile([P, MT, 2, HD], F32, name="tabq")
@@ -88,6 +90,7 @@ def tile_multiqueryattention_pa_kernel(
         nc.vector.memset(xs[:].bitcast(I32), 0)
         nc.vector.memset(zero[:], 0.0)
         nc.vector.memset(ws0[:].bitcast(I32), 0)
+        nc.vector.memset(ws1[:].bitcast(I32), 0)
         nc.vector.memset(wsr[:].bitcast(I32), 0)
 
         def load_codes(tile_ap, words, lo, hi):
@@ -110,8 +113,10 @@ def tile_multiqueryattention_pa_kernel(
         load_codes(wc[0][:], W_qkv_words, 0, 1024)
         load_scales(ws0, W_qkv_scales, 0, 512)
         load_codes(xcr[:], x_words, 256, 1024)
-        load_scales(wsr, W_qkv_scales, 512, 2304)
-        for c in range(1, QC):
+        load_scales(ws1, W_qkv_scales, 512, 1024)
+        load_codes(wc[1][:], W_qkv_words, 1024, 2048)
+        load_scales(wsr, W_qkv_scales, 1024, 2304)
+        for c in range(2, QC):
             load_codes(wc[c][:], W_qkv_words, 1024 * c, 1024 * (c + 1))
         load_codes(wckv[:], W_qkv_words, 4096, 4608)
 
@@ -171,8 +176,8 @@ def tile_multiqueryattention_pa_kernel(
                 parts[u].append((c, m, h0, nh))
                 acc = ps.tile([P, HD * nh], F32, tag="acc", name="acc%d_%d_%d" % (c, m, h0))
                 project(
-                    acc[:], m, wc[c], ws0 if c == 0 else wsr,
-                    (HD * h0, HD * h0 if c == 0 else 512 * (c - 1) + HD * h0), HD * nh,
+                    acc[:], m, wc[c], (ws0, ws1, wsr, wsr)[c],
+                    (HD * h0, (0, 0, 0, 512)[c] + HD * h0), HD * nh,
                 )
                 products(
                     blocks(acc[:]), tiles[u][:, off : off + nh, :, :],
@@ -184,12 +189,12 @@ def tile_multiqueryattention_pa_kernel(
                 parts[u] = None
                 acc = ps.tile([P, 512], F32, tag="acc", name="acc_k")
                 for m in range(MT):
-                    project(acc[:, HD * m : HD * (m + 1)], m, wckv, wsr, (0, 1536), HD)
+                    project(acc[:, HD * m : HD * (m + 1)], m, wckv, wsr, (0, 1024), HD)
                 products(blocks(acc[:]), tiles[u][:], tabk[:])
             elif st[0] == "v":
                 acc = ps.tile([P, 512], F32, tag="acc", name="acc_v")
                 for m in range(MT):
-                    project(acc[:, HD * m : HD * (m + 1)], m, wckv, wsr, (HD, 1664), HD)
+                    project(acc[:, HD * m : HD * (m + 1)], m, wckv, wsr, (HD, 1152), HD)
                 ov = sb.tile([P, 512], F32, name="ov")
                 nc.scalar.copy(out=ov[:], in_=acc[:])
                 nc.scalar.dma_start(out=out_2[0].rearrange("(m p) d -> p m d", p=P), in_=blocks(ov[:]))

@@ -73,13 +73,13 @@ def tile_multiqueryattention_pa_kernel(
         ctx.enter_context(tc.manual_schedule())
 
         xc0 = sb.tile([P, G, 256], U8, name="xc0", align_bytes=64)
-        xcr = sb.tile([P, G, 768], U8, name="xcr", align_bytes=64)
+        xc1 = sb.tile([P, G, 256], U8, name="xc1", align_bytes=64)
+        xcr = sb.tile([P, G, 512], U8, name="xcr", align_bytes=64)
         xs = sb.tile([P, G, T], U8, name="xs", align_bytes=64)
-        wc = [sb.tile([P, G, 1024], U8, name="wc%d" % c, align_bytes=64) for c in range(QC)]
-        wckv = sb.tile([P, G, 512], U8, name="wckv", align_bytes=64)
-        ws0 = sb.tile([P, G, 512], U8, name="ws0", align_bytes=64)
-        ws1 = sb.tile([P, G, 512], U8, name="ws1", align_bytes=64)
-        wsr = sb.tile([P, G, 1280], U8, name="wsr", align_bytes=64)
+        wc = [sb.tile([P, G, 1024], U8, name="wc%d" % c, align_bytes=64) for c in range(3)]
+        wc.append(sb.tile([P, G, 1536], U8, name="wc3kv", align_bytes=64))
+        ws = [sb.tile([P, G, 512], U8, name="ws%d" % c, align_bytes=64) for c in range(3)]
+        ws.append(sb.tile([P, G, 768], U8, name="ws3kv", align_bytes=64))
         cos_raw = sb.tile([P, MT, HD], BF16, name="cos_raw")
         sin_raw = sb.tile([P, MT, HD], BF16, name="sin_raw")
         tabq = sb.tile([P, MT, 2, HD], F32, name="tabq")
@@ -89,9 +89,8 @@ def tile_multiqueryattention_pa_kernel(
 
         nc.vector.memset(xs[:].bitcast(I32), 0)
         nc.vector.memset(zero[:], 0.0)
-        nc.vector.memset(ws0[:].bitcast(I32), 0)
-        nc.vector.memset(ws1[:].bitcast(I32), 0)
-        nc.vector.memset(wsr[:].bitcast(I32), 0)
+        for c in range(QC):
+            nc.vector.memset(ws[c][:].bitcast(I32), 0)
 
         def load_codes(tile_ap, words, lo, hi):
             nc.sync.dma_start(
@@ -99,11 +98,11 @@ def tile_multiqueryattention_pa_kernel(
                 in_=words[:, :, lo:hi].rearrange("g p n -> p g n").bitcast(I32),
             )
 
-        def load_scales(plane, scales, lo, hi, quads=(0, 1, 2, 3)):
-            for q in quads:
+        def load_scales(plane, scales, lo, hi):
+            for r in range(4):
                 nc.sync.dma_start(
-                    out=plane[32 * q : 32 * q + 4, :, :].bitcast(I32),
-                    in_=scales[:, 4 * q : 4 * q + 4, lo:hi].rearrange("g r n -> r g n").bitcast(I32),
+                    out=plane[r : P : 32, :, :].bitcast(I32),
+                    in_=scales[:, r : 16 : 4, lo:hi].rearrange("g q n -> q g n").bitcast(I32),
                 )
 
         load_codes(xc0[:], x_words, 0, 256)
@@ -111,14 +110,12 @@ def tile_multiqueryattention_pa_kernel(
         nc.scalar.dma_start(out=sin_raw[:], in_=sin.rearrange("(m p) d -> p m d", p=P))
         load_scales(xs, x_scales, 0, 512)
         load_codes(wc[0][:], W_qkv_words, 0, 1024)
-        load_scales(ws0, W_qkv_scales, 0, 512)
-        load_codes(xcr[:], x_words, 256, 1024)
-        load_scales(ws1, W_qkv_scales, 512, 1024)
-        load_codes(wc[1][:], W_qkv_words, 1024, 2048)
-        load_scales(wsr, W_qkv_scales, 1024, 2304)
-        for c in range(2, QC):
-            load_codes(wc[c][:], W_qkv_words, 1024 * c, 1024 * (c + 1))
-        load_codes(wckv[:], W_qkv_words, 4096, 4608)
+        load_scales(ws[0], W_qkv_scales, 0, 512)
+        load_codes(xc1[:], x_words, 256, 512)
+        load_codes(xcr[:], x_words, 512, 1024)
+        for c in range(1, QC):
+            load_scales(ws[c], W_qkv_scales, 512 * c, 512 * (c + 1) if c < 3 else 2304)
+            load_codes(wc[c][:], W_qkv_words, 1024 * c, 1024 * (c + 1) if c < 3 else 4608)
 
         if WARM:
             warm = ps.tile([P, 512], F32, tag="acc", name="warm")
@@ -135,7 +132,7 @@ def tile_multiqueryattention_pa_kernel(
             for g in range(G):
                 nc.tensor.matmul_mx(
                     out=acc,
-                    lhsT=(xc0[:, g, :] if m == 0 else xcr[:, g, 256 * (m - 1) : 256 * m]).bitcast(FP4X4),
+                    lhsT=(xc0[:, g, :], xc1[:, g, :], xcr[:, g, 0:256], xcr[:, g, 256:512])[m].bitcast(FP4X4),
                     lhsT_scale=xs[:, g, P * m : P * (m + 1)],
                     rhs=codes[:, g, 2 * col[0] : 2 * (col[0] + n)].bitcast(FP4X4),
                     rhs_scale=plane[:, g, col[1] : col[1] + n],
@@ -176,8 +173,7 @@ def tile_multiqueryattention_pa_kernel(
                 parts[u].append((c, m, h0, nh))
                 acc = ps.tile([P, HD * nh], F32, tag="acc", name="acc%d_%d_%d" % (c, m, h0))
                 project(
-                    acc[:], m, wc[c], (ws0, ws1, wsr, wsr)[c],
-                    (HD * h0, (0, 0, 0, 512)[c] + HD * h0), HD * nh,
+                    acc[:], m, wc[c], ws[c], (HD * h0, HD * h0), HD * nh,
                 )
                 products(
                     blocks(acc[:]), tiles[u][:, off : off + nh, :, :],
@@ -189,12 +185,12 @@ def tile_multiqueryattention_pa_kernel(
                 parts[u] = None
                 acc = ps.tile([P, 512], F32, tag="acc", name="acc_k")
                 for m in range(MT):
-                    project(acc[:, HD * m : HD * (m + 1)], m, wckv, wsr, (0, 1024), HD)
+                    project(acc[:, HD * m : HD * (m + 1)], m, wc[3], ws[3], (512, 512), HD)
                 products(blocks(acc[:]), tiles[u][:], tabk[:])
             elif st[0] == "v":
                 acc = ps.tile([P, 512], F32, tag="acc", name="acc_v")
                 for m in range(MT):
-                    project(acc[:, HD * m : HD * (m + 1)], m, wckv, wsr, (HD, 1152), HD)
+                    project(acc[:, HD * m : HD * (m + 1)], m, wc[3], ws[3], (640, 640), HD)
                 ov = sb.tile([P, 512], F32, name="ov")
                 nc.scalar.copy(out=ov[:], in_=acc[:])
                 nc.scalar.dma_start(out=out_2[0].rearrange("(m p) d -> p m d", p=P), in_=blocks(ov[:]))

@@ -47,17 +47,19 @@ STEPS = [
     ("q", "h", 2, 2, 0, 4),
     ("q", "h", 2, 3, 0, 4),
     ("sum", "g", "h", "s"),
+    ("v",),
     ("k", "k"),
     ("sum", "g", "k", "a"),
     ("q", "i", 3, 0, 0, 4),
     ("sum", "g", "i", "s"),
     ("q", "m", 3, 1, 0, 4),
     ("sum", "g", "m", "s"),
-    ("q", "j", 3, 2, 0, 4),
+    ("q", "j", 3, 2, 0, 2),
+    ("sum", "g", "j", "s"),
+    ("q", "r", 3, 2, 2, 2),
     ("q", "l", 3, 3, 0, 2),
     ("q", "n", 3, 3, 2, 2),
-    ("v",),
-    ("sum", "v", "j", "a"),
+    ("sum", "v", "r", "a"),
     ("sum", "v", "l", "a"),
     ("sum", "v", "n", "a"),
 ]

@@ -74,14 +74,14 @@ def tile_multiqueryattention_pa_kernel(
         ps = ctx.enter_context(tc.psum_pool(name="ps", bufs=8))
         ctx.enter_context(tc.manual_schedule())
 
-        xc0 = sb.tile([P, G, 256], U8, name="xc0", align_bytes=64)
-        xc1 = sb.tile([P, G, 256], U8, name="xc1", align_bytes=64)
-        xcr = sb.tile([P, G, 512], U8, name="xcr", align_bytes=64)
-        xs = sb.tile([P, G, T], U8, name="xs", align_bytes=64)
-        wc = [sb.tile([P, G, 1024], U8, name="wc%d" % c, align_bytes=64) for c in range(3)]
-        wc.append(sb.tile([P, G, 1536], U8, name="wc3kv", align_bytes=64))
-        ws = [sb.tile([P, G, 512], U8, name="ws%d" % c, align_bytes=64) for c in range(3)]
-        ws.append(sb.tile([P, G, 768], U8, name="ws3kv", align_bytes=64))
+        xc0 = sb.tile([P, G, 256], U8, name="xc0", align_bytes=256)
+        xc1 = sb.tile([P, G, 256], U8, name="xc1", align_bytes=256)
+        xcr = sb.tile([P, G, 512], U8, name="xcr", align_bytes=256)
+        xs = sb.tile([P, G, T], U8, name="xs", align_bytes=256)
+        wc = [sb.tile([P, G, 1024], U8, name="wc%d" % c, align_bytes=256) for c in range(3)]
+        wc.append(sb.tile([P, G, 1536], U8, name="wc3kv", align_bytes=256))
+        ws = [sb.tile([P, G, 512], U8, name="ws%d" % c, align_bytes=256) for c in range(3)]
+        ws.append(sb.tile([P, G, 768], U8, name="ws3kv", align_bytes=256))
         cos_raw = sb.tile([P, MT, HD], BF16, name="cos_raw")
         sin_raw = sb.tile([P, MT, HD], BF16, name="sin_raw")
         tabq = sb.tile([P, MT, 2, HD], F32, name="tabq")

@@ -82,8 +82,8 @@ def tile_multiqueryattention_pa_kernel(
         wc.append(sb.tile([P, G, 1536], U8, name="wc3kv", align_bytes=256))
         ws = [sb.tile([P, G, 512], U8, name="ws%d" % c, align_bytes=256) for c in range(3)]
         ws.append(sb.tile([P, G, 768], U8, name="ws3kv", align_bytes=256))
-        cos_raw = sb.tile([P, MT, HD], BF16, name="cos_raw")
-        sin_raw = sb.tile([P, MT, HD], BF16, name="sin_raw")
+        cos_raw = sb.tile([P, MT, HD], BF16, name="cos_raw", align_bytes=256)
+        sin_raw = sb.tile([P, MT, HD], BF16, name="sin_raw", align_bytes=256)
         tabq = sb.tile([P, MT, 2, HD], F32, name="tabq")
         tabk = sb.tile([P, MT, 2, HD], F32, name="tabk")
         zero = sb.tile([P, 512], BF16, name="zero")
@@ -193,13 +193,13 @@ def tile_multiqueryattention_pa_kernel(
                 acc = ps.tile([P, 512], F32, tag="acc", name="acc_v")
                 for m in range(MT):
                     project(acc[:, HD * m : HD * (m + 1)], m, wc[3], ws[3], (640, 640), HD)
-                ov = sb.tile([P, 512], F32, name="ov")
+                ov = sb.tile([P, 512], F32, name="ov", align_bytes=256)
                 nc.scalar.copy(out=ov[:], in_=acc[:])
                 nc.scalar.dma_start(out=out_2[0].rearrange("(m p) d -> p m d", p=P), in_=blocks(ov[:]))
             else:
                 (kind, eng, u, qu) = st
                 dma = nc.sync if qu == "s" else nc.scalar
-                o = sb.tile([P, size[u], HD], F32, name="o_%s" % u)
+                o = sb.tile([P, size[u], HD], F32, name="o_%s" % u, align_bytes=256)
                 rope_sum(nc.vector if eng == "v" else nc.gpsimd, o[:], tiles[u])
                 if parts[u] is None:
                     dma.dma_start(out=out_1[0].rearrange("(m p) d -> p m d", p=P), in_=o[:])

@@ -29,15 +29,18 @@ STEPS = [
     ("sum", "g", "a", "s"),
     ("q", "b", 0, 0, 2, 2),
     ("sum", "g", "b", "s"),
-    ("q", "c", 0, 1, 0, 4),
+    ("q", "c", 0, 1, 0, 2),
     ("sum", "g", "c", "s"),
+    ("q", "c2", 0, 1, 2, 2),
+    ("sum", "g", "c2", "s"),
     ("q", "d", 0, 2, 0, 4),
     ("sum", "g", "d", "s"),
     ("q", "p", 0, 3, 0, 4),
     ("sum", "g", "p", "s"),
     ("q", "e", 1, 0, 0, 4),
-    ("q", "e", 1, 1, 0, 4),
     ("sum", "g", "e", "s"),
+    ("q", "e2", 1, 1, 0, 4),
+    ("sum", "g", "e2", "s"),
     ("q", "f", 1, 2, 0, 4),
     ("q", "f", 1, 3, 0, 4),
     ("sum", "g", "f", "s"),
@@ -47,19 +50,18 @@ STEPS = [
     ("q", "h", 2, 2, 0, 4),
     ("q", "h", 2, 3, 0, 4),
     ("sum", "g", "h", "s"),
-    ("v",),
-    ("k", "k"),
-    ("sum", "g", "k", "a"),
     ("q", "i", 3, 0, 0, 4),
     ("sum", "g", "i", "s"),
     ("q", "m", 3, 1, 0, 4),
     ("sum", "g", "m", "s"),
-    ("q", "j", 3, 2, 0, 2),
+    ("q", "j", 3, 2, 0, 4),
     ("sum", "g", "j", "s"),
-    ("q", "r", 3, 2, 2, 2),
+    ("kv", "k", 0),
+    ("kv", "k", 1),
+    ("vstore",),
     ("q", "l", 3, 3, 0, 2),
     ("q", "n", 3, 3, 2, 2),
-    ("sum", "v", "r", "a"),
+    ("sum", "v", "k", "a"),
     ("sum", "v", "l", "a"),
     ("sum", "v", "n", "a"),
 ]
@@ -161,16 +163,17 @@ def tile_multiqueryattention_pa_kernel(
         for st in STEPS:
             if st[0] == "q":
                 size[st[1]] = size.get(st[1], 0) + st[5]
-            elif st[0] == "k":
-                size[st[1]] = MT
+            elif st[0] == "kv":
+                size[st[1]] = size.get(st[1], 0) + 2
         tiles = {}
         parts = {}
+        ov = sb.tile([P, MT, HD], F32, name="ov", align_bytes=256)
         for st in STEPS:
+            if st[0] in ("q", "kv") and st[1] not in tiles:
+                tiles[st[1]] = sb.tile([P, size[st[1]], 2, HD], F32, name="ab_%s" % st[1])
+                parts[st[1]] = []
             if st[0] == "q":
                 (kind, u, c, m, h0, nh) = st
-                if u not in tiles:
-                    tiles[u] = sb.tile([P, size[u], 2, HD], F32, name="ab_%s" % u)
-                    parts[u] = []
                 off = sum(p[3] for p in parts[u])
                 parts[u].append((c, m, h0, nh))
                 acc = ps.tile([P, HD * nh], F32, tag="acc", name="acc%d_%d_%d" % (c, m, h0))
@@ -181,35 +184,34 @@ def tile_multiqueryattention_pa_kernel(
                     blocks(acc[:]), tiles[u][:, off : off + nh, :, :],
                     tabq[:, m, :, :].unsqueeze(1).to_broadcast([P, nh, 2, HD]),
                 )
-            elif st[0] == "k":
-                u = st[1]
-                tiles[u] = sb.tile([P, MT, 2, HD], F32, name="ab_%s" % u)
-                parts[u] = None
-                acc = ps.tile([P, 512], F32, tag="acc", name="acc_k")
-                for m in range(MT):
-                    project(acc[:, HD * m : HD * (m + 1)], m, wc[3], ws[3], (512, 512), HD)
-                products(blocks(acc[:]), tiles[u][:], tabk[:])
-            elif st[0] == "v":
-                acc = ps.tile([P, 512], F32, tag="acc", name="acc_v")
-                for m in range(MT):
-                    project(acc[:, HD * m : HD * (m + 1)], m, wc[3], ws[3], (640, 640), HD)
-                ov = sb.tile([P, 512], F32, name="ov", align_bytes=256)
-                nc.scalar.copy(out=ov[:], in_=acc[:])
-                nc.scalar.dma_start(out=out_2[0].rearrange("(m p) d -> p m d", p=P), in_=blocks(ov[:]))
+            elif st[0] == "kv":
+                (kind, u, j) = st
+                off = sum(p[3] for p in parts[u])
+                parts[u].append((None, 2 * j, 0, 2))
+                acc = ps.tile([P, 512], F32, tag="acc", name="acc_kv%d" % j)
+                for t in range(2):
+                    project(acc[:, 256 * t : 256 * (t + 1)], 2 * j + t, wc[3], ws[3], (512, 512), 256)
+                both = acc[:].rearrange("p (t s d) -> p t s d", s=2, d=HD)
+                products(both[:, :, 0, :], tiles[u][:, off : off + 2, :, :], tabk[:, 2 * j : 2 * j + 2, :, :])
+                nc.scalar.copy(out=ov[:, 2 * j : 2 * j + 2, :], in_=both[:, :, 1, :])
+            elif st[0] == "vstore":
+                nc.scalar.dma_start(out=out_2[0].rearrange("(m p) d -> p m d", p=P), in_=ov[:])
             else:
                 (kind, eng, u, qu) = st
                 dma = nc.sync if qu == "s" else nc.scalar
                 o = sb.tile([P, size[u], HD], F32, name="o_%s" % u, align_bytes=256)
                 rope_sum(nc.vector if eng == "v" else nc.gpsimd, o[:], tiles[u])
-                if parts[u] is None:
-                    dma.dma_start(out=out_1[0].rearrange("(m p) d -> p m d", p=P), in_=o[:])
-                else:
-                    off = 0
-                    for (c, m, h0, nh) in parts[u]:
-                        dma.dma_start(
-                            out=out_0[0, 4 * c + h0 : 4 * c + h0 + nh, P * m : P * (m + 1), :].rearrange(
-                                "h p d -> p h d"
-                            ),
-                            in_=o[:, off : off + nh, :],
-                        )
-                        off += nh
+                merged = []
+                for (c, m, h0, nh) in parts[u]:
+                    if merged and c is None and merged[-1][0] is None:
+                        merged[-1] = (None, merged[-1][1], 0, merged[-1][3] + nh)
+                    else:
+                        merged.append((c, m, h0, nh))
+                off = 0
+                for (c, m, h0, nh) in merged:
+                    if c is None:
+                        dest = out_1[0, P * m : P * (m + nh), :].rearrange("(m p) d -> p m d", p=P)
+                    else:
+                        dest = out_0[0, 4 * c + h0 : 4 * c + h0 + nh, P * m : P * (m + 1), :].rearrange("h p d -> p h d")
+                    dma.dma_start(out=dest, in_=o[:, off : off + nh, :])
+                    off += nh

@@ -55,14 +55,14 @@ STEPS = [
     ("q", "m", 3, 1, 0, 4),
     ("sum", "g", "m", "s"),
     ("q", "j", 3, 2, 0, 4),
-    ("sum", "g", "j", "s"),
     ("kv", "k", 0),
     ("kv", "k", 1),
     ("vstore",),
     ("q", "l", 3, 3, 0, 2),
     ("q", "n", 3, 3, 2, 2),
+    ("sum", "v", "j", "s"),
     ("sum", "v", "k", "a"),
-    ("sum", "v", "l", "a"),
+    ("sum", "v", "l", "s"),
     ("sum", "v", "n", "a"),
 ]
 

@@ -170,7 +170,8 @@ def tile_multiqueryattention_pa_kernel(
         ov = sb.tile([P, MT, HD], F32, name="ov", align_bytes=256)
         for st in STEPS:
             if st[0] in ("q", "kv") and st[1] not in tiles:
-                tiles[st[1]] = sb.tile([P, size[st[1]], 2, HD], F32, name="ab_%s" % st[1])
+                raw = sb.tile([P, size[st[1]] * 2 * HD + 64], F32, name="ab_%s" % st[1], align_bytes=256)
+                tiles[st[1]] = raw[:, 8 : 8 + size[st[1]] * 2 * HD].rearrange("p (h s d) -> p h s d", s=2, d=HD)
                 parts[st[1]] = []
             if st[0] == "q":
                 (kind, u, c, m, h0, nh) = st

from contextlib import ExitStack

import concourse.mybir as mybir

F32 = mybir.dt.float32
BF16 = mybir.dt.bfloat16
I32 = mybir.dt.int32
U8 = mybir.dt.uint8
FP4X4 = mybir.dt.float4_e2m1fn_x4
MULT = mybir.AluOpType.mult
ADD = mybir.AluOpType.add
COPY = mybir.ActivationFunctionType.Copy

P = 128
T = 512
D = 2048
HD = 128
HALF = 64
G = 4
MT = 4
QC = 4
SCALE = HD ** -0.5
FLOPS = 2 * T * D * (D + 2 * HD)

WARM = 12

STEPS = [
    ("q", "a", 0, 0, 0, 2),
    ("sum", "g", "a", "s"),
    ("q", "b", 0, 0, 2, 2),
    ("sum", "g", "b", "s"),
    ("q", "c", 0, 1, 0, 2),
    ("sum", "g", "c", "s"),
    ("q", "c2", 0, 1, 2, 2),
    ("sum", "g", "c2", "s"),
    ("q", "d", 0, 2, 0, 4),
    ("sum", "g", "d", "s"),
    ("q", "p", 0, 3, 0, 4),
    ("sum", "g", "p", "s"),
    ("q", "e", 1, 0, 0, 4),
    ("sum", "g", "e", "s"),
    ("q", "e2", 1, 1, 0, 4),
    ("sum", "g", "e2", "s"),
    ("q", "f", 1, 2, 0, 4),
    ("q", "f", 1, 3, 0, 4),
    ("sum", "g", "f", "s"),
    ("q", "g", 2, 0, 0, 4),
    ("q", "g", 2, 1, 0, 4),
    ("sum", "g", "g", "s"),
    ("q", "h", 2, 2, 0, 4),
    ("q", "h", 2, 3, 0, 4),
    ("sum", "g", "h", "s"),
    ("q", "i", 3, 0, 0, 4),
    ("sum", "g", "i", "s"),
    ("q", "m", 3, 1, 0, 4),
    ("sum", "g", "m", "s"),
    ("q", "j", 3, 2, 0, 4),
    ("kv", "k", 0),
    ("kv", "k", 1),
    ("vstore",),
    ("q", "l", 3, 3, 0, 2),
    ("q", "n", 3, 3, 2, 2),
    ("sum", "v", "j", "s"),
    ("sum", "v", "k", "a"),
    ("sum", "v", "l", "s"),
    ("sum", "v", "n", "a"),
]


def tile_multiqueryattention_pa_kernel(
    tc, x_words, x_scales, sin, cos, W_qkv_words, W_qkv_scales, out_0, out_1, out_2
):
    nc = tc.nc
    with ExitStack() as ctx:
        sb = ctx.enter_context(tc.tile_pool(name="sb", bufs=1))
        ps = ctx.enter_context(tc.psum_pool(name="ps", bufs=8))
        ctx.enter_context(tc.manual_schedule())

        xc0 = sb.tile([P, G, 256], U8, name="xc0", align_bytes=256)
        xc1 = sb.tile([P, G, 256], U8, name="xc1", align_bytes=256)
        xcr = sb.tile([P, G, 512], U8, name="xcr", align_bytes=256)
        xs = sb.tile([P, G, T], U8, name="xs", align_bytes=256)
        wc = [sb.tile([P, G, 1024], U8, name="wc%d" % c, align_bytes=256) for c in range(3)]
        wc.append(sb.tile([P, G, 1536], U8, name="wc3kv", align_bytes=256))
        ws = [sb.tile([P, G, 512], U8, name="ws%d" % c, align_bytes=256) for c in range(3)]
        ws.append(sb.tile([P, G, 768], U8, name="ws3kv", align_bytes=256))
        cos_raw = sb.tile([P, MT, HD], BF16, name="cos_raw", align_bytes=256)
        sin_raw = sb.tile([P, MT, HD], BF16, name="sin_raw", align_bytes=256)
        tabq = sb.tile([P, MT, 2, HD], F32, name="tabq")
        tabk = sb.tile([P, MT, 2, HD], F32, name="tabk")
        zero = sb.tile([P, 512], BF16, name="zero")
        scr = sb.tile([P, 8], F32, name="scr")

        nc.vector.memset(xs[:].bitcast(I32), 0)
        nc.vector.memset(zero[:], 0.0)
        for c in range(QC):
            nc.vector.memset(ws[c][:].bitcast(I32), 0)

        def load_codes(tile_ap, words, lo, hi):
            nc.sync.dma_start(
                out=tile_ap.bitcast(I32),
                in_=words[:, :, lo:hi].rearrange("g p n -> p g n").bitcast(I32),
            )

        def load_scales(plane, scales, lo, hi):
            for r in range(4):
                nc.sync.dma_start(
                    out=plane[r : P : 32, :, :].bitcast(I32),
                    in_=scales[:, r : 16 : 4, lo:hi].rearrange("g q n -> q g n").bitcast(I32),
                )

        load_codes(xc0[:], x_words, 0, 256)
        nc.scalar.dma_start(out=cos_raw[:], in_=cos.rearrange("(m p) d -> p m d", p=P))
        nc.scalar.dma_start(out=sin_raw[:], in_=sin.rearrange("(m p) d -> p m d", p=P))
        load_scales(xs, x_scales, 0, 512)
        load_codes(wc[0][:], W_qkv_words, 0, 1024)
        load_scales(ws[0], W_qkv_scales, 0, 512)
        load_codes(xc1[:], x_words, 256, 512)
        load_codes(xcr[:], x_words, 512, 1024)
        for c in range(1, QC):
            load_scales(ws[c], W_qkv_scales, 512 * c, 512 * (c + 1) if c < 3 else 2304)
            load_codes(wc[c][:], W_qkv_words, 1024 * c, 1024 * (c + 1) if c < 3 else 4608)

        if WARM:
            warm = ps.tile([P, 512], F32, tag="acc", name="warm")
            for i in range(WARM):
                nc.tensor.matmul(out=warm[:], lhsT=zero[:, 0:P], rhs=zero[:], start=True, stop=True)

        nc.scalar.activation(out=scr[:, 0:1], in_=zero[:, 0:1], func=COPY, scale=1.0)
        for (tab, f) in ((tabq, SCALE), (tabk, 1.0)):
            nc.scalar.activation(out=tab[:, :, 0, :], in_=cos_raw[:], func=COPY, scale=f)
            nc.scalar.activation(out=tab[:, :, 1, 0:HALF], in_=sin_raw[:, :, HALF:HD], func=COPY, scale=f)
            nc.scalar.activation(out=tab[:, :, 1, HALF:HD], in_=sin_raw[:, :, 0:HALF], func=COPY, scale=-f)

        def project(acc, m, codes, plane, col, n):
            for g in range(G):
                nc.tensor.matmul_mx(
                    out=acc,
                    lhsT=(xc0[:, g, :], xc1[:, g, :], xcr[:, g, 0:256], xcr[:, g, 256:512])[m].bitcast(FP4X4),
                    lhsT_scale=xs[:, g, P * m : P * (m + 1)],
                    rhs=codes[:, g, 2 * col[0] : 2 * (col[0] + n)].bitcast(FP4X4),
                    rhs_scale=plane[:, g, col[1] : col[1] + n],
                    start=(g == 0),
                    stop=(g == G - 1),
                )

        def blocks(ap):
            return ap.rearrange("p (h d) -> p h d", d=HD)

        def products(acc, ab, tab):
            nb = acc.shape[1]
            nc.vector.tensor_tensor(out=ab, in0=acc.unsqueeze(2).to_broadcast([P, nb, 2, HD]), in1=tab, op=MULT)

        def halves(ap):
            return ap.rearrange("p h (s d) -> p h s d", s=2)

        def rope_sum(eng, o, ab):
            eng.tensor_tensor(
                out=halves(o), in0=halves(ab[:, :, 0, :]), in1=halves(ab[:, :, 1, :])[:, :, ::-1, :], op=ADD
            )

        size = {}
        for st in STEPS:
            if st[0] == "q":
                size[st[1]] = size.get(st[1], 0) + st[5]
            elif st[0] == "kv":
                size[st[1]] = size.get(st[1], 0) + 2
        tiles = {}
        parts = {}
        ov = sb.tile([P, MT, HD], F32, name="ov", align_bytes=256)
        for st in STEPS:
            if st[0] in ("q", "kv") and st[1] not in tiles:
                raw = sb.tile([P, size[st[1]] * 2 * HD + 64], F32, name="ab_%s" % st[1], align_bytes=256)
                tiles[st[1]] = raw[:, 8 : 8 + size[st[1]] * 2 * HD].rearrange("p (h s d) -> p h s d", s=2, d=HD)
                parts[st[1]] = []
            if st[0] == "q":
                (kind, u, c, m, h0, nh) = st
                off = sum(p[3] for p in parts[u])
                parts[u].append((c, m, h0, nh))
                acc = ps.tile([P, HD * nh], F32, tag="acc", name="acc%d_%d_%d" % (c, m, h0))
                project(
                    acc[:], m, wc[c], ws[c], (HD * h0, HD * h0), HD * nh,
                )
                products(
                    blocks(acc[:]), tiles[u][:, off : off + nh, :, :],
                    tabq[:, m, :, :].unsqueeze(1).to_broadcast([P, nh, 2, HD]),
                )
            elif st[0] == "kv":
                (kind, u, j) = st
                off = sum(p[3] for p in parts[u])
                parts[u].append((None, 2 * j, 0, 2))
                acc = ps.tile([P, 512], F32, tag="acc", name="acc_kv%d" % j)
                for t in range(2):
                    project(acc[:, 256 * t : 256 * (t + 1)], 2 * j + t, wc[3], ws[3], (512, 512), 256)
                both = acc[:].rearrange("p (t s d) -> p t s d", s=2, d=HD)
                products(both[:, :, 0, :], tiles[u][:, off : off + 2, :, :], tabk[:, 2 * j : 2 * j + 2, :, :])
                nc.scalar.copy(out=ov[:, 2 * j : 2 * j + 2, :], in_=both[:, :, 1, :])
            elif st[0] == "vstore":
                nc.scalar.dma_start(out=out_2[0].rearrange("(m p) d -> p m d", p=P), in_=ov[:])
            else:
                (kind, eng, u, qu) = st
                dma = nc.sync if qu == "s" else nc.scalar
                o = sb.tile([P, size[u], HD], F32, name="o_%s" % u, align_bytes=256)
                rope_sum(nc.vector if eng == "v" else nc.gpsimd, o[:], tiles[u])
                merged = []
                for (c, m, h0, nh) in parts[u]:
                    if merged and c is None and merged[-1][0] is None:
                        merged[-1] = (None, merged[-1][1], 0, merged[-1][3] + nh)
                    else:
                        merged.append((c, m, h0, nh))
                off = 0
                for (c, m, h0, nh) in merged:
                    if c is None:
                        dest = out_1[0, P * m : P * (m + nh), :].rearrange("(m p) d -> p m d", p=P)
                    else:
                        dest = out_0[0, 4 * c + h0 : 4 * c + h0 + nh, P * m : P * (m + 1), :].rearrange("h p d -> p h d")
                    dma.dma_start(out=dest, in_=o[:, off : off + nh, :])
                    off += nh
